import numpy as np
import ml_dtypes


def mxq(x, axis, fmt="e4m3"):
    dtype, down = {"e4m3": (ml_dtypes.float8_e4m3fn, 7), "e5m2": (ml_dtypes.float8_e5m2, 14)}[fmt]
    v = np.moveaxis(np.asarray(x, np.float32).astype(ml_dtypes.bfloat16).astype(np.float64), axis, -1)
    blocks = v.reshape(v.shape[:-1] + (-1, 32))
    amax = np.abs(blocks).max(-1, keepdims=True)
    byte = np.maximum(np.where(amax > 0, np.frexp(amax)[1] - 1 + 127, 0) - down, 1)
    scale = np.exp2(byte - 127.0)
    codes = (blocks / scale).astype(np.float32).astype(dtype).astype(np.float64)
    return np.moveaxis((codes * scale).reshape(v.shape), -1, axis)


WIDE = False


def mx_kscale(k):
    if not WIDE:
        return np.ones(k)
    levels = np.array([10, -10, 5, -5, 0])
    a = np.random.permutation(np.resize(levels, k // 512 * 4)).reshape(k // 512, 4)
    idx = np.arange(k)
    return np.exp2(a[idx // 512, idx % 128 // 32])


BF16 = ml_dtypes.bfloat16


def bf(x):
    return np.asarray(x, np.float32).astype(BF16)


def f64(x):
    return np.asarray(x).astype(np.float64)


B, C_IN, C_OUT, K_SIZE, STRIDE, PAD, H = 2, 512, 128, 3, 1, 1, 56
H_OUT = (H + 2 * PAD - K_SIZE) // STRIDE + 1
KK = C_IN * K_SIZE * K_SIZE
BLK = 32
RUN = int(np.lcm(BLK, K_SIZE * K_SIZE)) // (K_SIZE * K_SIZE)


def setup_inputs():
    s = mx_kscale(KK)
    sc = s[(np.arange(C_IN) // RUN) * RUN * K_SIZE * K_SIZE]
    sf = np.repeat(sc, K_SIZE * K_SIZE)
    x = np.random.standard_normal((B, C_IN, H, H)) * sc[None, :, None, None]
    Kf = np.random.uniform(-1.0, 1.0, (KK, C_OUT)) * np.sqrt(3.0 / KK) / sf[:, None]
    return {"x": bf(x), "K": bf(Kf.reshape(K_SIZE, K_SIZE, C_IN, C_OUT))}


def reference(x, K):
    xp = np.pad(f64(x), ((0, 0), (0, 0), (PAD, PAD), (PAD, PAD)))
    end = (H_OUT - 1) * STRIDE + 1
    rows = []
    for di in range(K_SIZE):
        cols = []
        for dj in range(K_SIZE):
            cols.append(xp[:, :, di:di + end:STRIDE, dj:dj + end:STRIDE])
        rows.append(np.stack(cols, axis=2))
    patches = np.stack(rows, axis=2)
    p = patches.transpose(0, 4, 5, 1, 2, 3).reshape(B, H_OUT, H_OUT, -1)
    Kf = f64(K).reshape(-1, C_OUT)
    out = mxq(p, 3, "e4m3") @ mxq(Kf, 0, "e4m3")
    return out.transpose(0, 3, 1, 2)

@@ -1,0 +1,194 @@
+from contextlib import ExitStack
+
+import concourse.mybir as mybir
+
+BF16 = mybir.dt.bfloat16
+F32 = mybir.dt.float32
+U32 = mybir.dt.uint32
+U8 = mybir.dt.uint8
+FP8X4 = mybir.dt.float8_e4m3fn_x4
+
+P = 128
+PACK = 4
+NB = 2
+C_OUT = 128
+H = 56
+W = 56
+RP = H + 2
+NPX = H * W
+TAPS = 9
+CH_ROWS = 8
+N_CH = H // CH_ROWS
+LEAD = 1
+
+FLOPS = 2 * NB * NPX * 512 * TAPS * C_OUT
+
+GROUPS_B0 = [128, 256, 512, 512, 512, 512, 512, 128]
+GROUPS_B1 = [512, 512, 512, 512, 512, 256, 128, 128]
+LEFT = 64
+
+
+def tile_conv2d_kernel(tc, x, K, out):
+    nc = tc.nc
+    with ExitStack() as ctx:
+        keep = ctx.enter_context(tc.tile_pool(name="keep", bufs=1))
+        wpool = ctx.enter_context(tc.tile_pool(name="wpool", bufs=6))
+        opool = ctx.enter_context(tc.tile_pool(name="opool", bufs=4))
+        psum = ctx.enter_context(tc.psum_pool(name="psum", bufs=8))
+
+        raw = {}
+        kraw = keep.tile([P, PACK, TAPS * C_OUT], BF16, name="kraw")
+
+        def load_chunk(b, k):
+            t = keep.tile([P, PACK, CH_ROWS * W], BF16, name="raw%d_%d" % (b, k))
+            r0 = k * CH_ROWS
+            nc.sync.dma_start(
+                out=t[:],
+                in_=x[b, :, r0 : r0 + CH_ROWS, :].rearrange("(p t) r c -> p t (r c)", t=PACK),
+            )
+            raw[(b, k)] = t
+
+        load_chunk(0, 0)
+        nc.sync.dma_start(
+            out=kraw[:].rearrange("p t f -> p (t f)"),
+            in_=K.rearrange("a b c o -> (a b c) o").rearrange("(p f) o -> p (f o)", p=P),
+        )
+        for b in range(NB):
+            for k in range(N_CH):
+                if (b, k) != (0, 0):
+                    load_chunk(b, k)
+
+        g = [keep.tile([P, RP * W, PACK], BF16, align_bytes=64, name="g%d" % dj) for dj in range(3)]
+        grow = [t[:].rearrange("p (r j) t -> p r (j t)", j=W) for t in g]
+        for dj in range(3):
+            nc.vector.memset(grow[dj][:, 0:1, :], 0.0)
+            nc.vector.memset(grow[dj][:, RP - 1 : RP, :], 0.0)
+        nc.vector.memset(grow[0][:, 1 : RP - 1, 0 : 4 * PACK], 0.0)
+        nc.vector.memset(grow[2][:, 1 : RP - 1, (W - 4) * PACK : W * PACK], 0.0)
+
+        def prep_chunk(b, k, on_vector):
+            ra = k * CH_ROWS + 1
+            rb = ra + CH_ROWS
+            dst = g[1][:, ra * W : rb * W, :].rearrange("p (c i) t -> p c t i", i=4)
+            src = raw[(b, k)][:].rearrange("p t (c i) -> p c t i", i=4)
+            last = (W - 1) * PACK
+            if on_vector:
+                nc.vector.tensor_copy(out=dst, in_=src)
+                nc.vector.tensor_copy(out=grow[0][:, ra:rb, PACK:], in_=grow[1][:, ra:rb, 0:last])
+                nc.vector.tensor_copy(out=grow[2][:, ra:rb, 0:last], in_=grow[1][:, ra:rb, PACK:])
+            else:
+                nc.scalar.copy(out=dst, in_=src)
+                nc.scalar.copy(out=grow[0][:, ra:rb, PACK:], in_=grow[1][:, ra:rb, 0:last])
+                nc.scalar.copy(out=grow[2][:, ra:rb, 0:last], in_=grow[1][:, ra:rb, PACK:])
+
+        kg = keep.tile([P, TAPS * C_OUT, PACK], BF16, align_bytes=64, name="kg")
+        kw = keep.tile([P, TAPS * C_OUT], U32, align_bytes=64, name="kw")
+        ks = keep.tile([P, TAPS * C_OUT], U8, align_bytes=64, name="ks")
+
+        def prep_weights():
+            nc.vector.tensor_copy(
+                out=kg[:].rearrange("p (c i) t -> p c t i", i=4),
+                in_=kraw[:].rearrange("p t (c i) -> p c t i", i=4),
+            )
+            for c0, c1 in ((0, 1024), (1024, 1152)):
+                nc.vector.quantize_mx(
+                    out=kw[:, c0:c1].bitcast(FP8X4),
+                    scales=ks[:, c0:c1],
+                    in_=kg[:, c0:c1, :].rearrange("p c t -> p (c t)"),
+                )
+
+        def quantise(dst_w, dst_s, s, q0, n):
+            di, dj = divmod(s, 3)
+            a = q0 + W * di
+            nc.vector.quantize_mx(
+                out=dst_w.bitcast(FP8X4),
+                scales=dst_s,
+                in_=g[dj][:, a : a + n, :].rearrange("p q t -> p (q t)"),
+            )
+
+        def multiply(acc, src_w, src_s, s):
+            nc.tensor.matmul_mx(
+                out=acc,
+                lhsT=kw[:, s * C_OUT : (s + 1) * C_OUT].bitcast(FP8X4),
+                lhsT_scale=ks[:, s * C_OUT : (s + 1) * C_OUT],
+                rhs=src_w.bitcast(FP8X4),
+                rhs_scale=src_s,
+                start=(s == 0),
+                stop=(s == TAPS - 1),
+            )
+
+        out_flat = [out[b].rearrange("o i j -> o (i j)") for b in range(NB)]
+
+        def group(b, q0, n):
+            acc = psum.tile([P, n], F32, tag="acc", name="acc")
+            for s in range(TAPS):
+                w = wpool.tile([P, n], U32, align_bytes=64, tag="w", name="w")
+                sc = wpool.tile([P, n], U8, align_bytes=64, tag="sc", name="sc")
+                quantise(w[:], sc[:], s, q0, n)
+                multiply(acc[:], w[:], sc[:], s)
+            res = opool.tile([P, n], F32, tag="res", name="res")
+            nc.scalar.copy(out=res[:], in_=acc[:])
+            nc.sync.dma_start(out=out_flat[b][:, q0 : q0 + n], in_=res[:])
+
+        lw = keep.tile([P, TAPS, 2 * LEFT], U32, align_bytes=64, name="lw")
+        ls = keep.tile([P, TAPS, 2 * LEFT], U8, align_bytes=64, name="ls")
+
+        def left_quantise(b, q0):
+            for s in range(TAPS):
+                quantise(lw[:, s, b * LEFT : (b + 1) * LEFT], ls[:, s, b * LEFT : (b + 1) * LEFT], s, q0, LEFT)
+
+        def left_finish(q_of_b):
+            acc = psum.tile([P, 2 * LEFT], F32, tag="acc", name="acc")
+            for s in range(TAPS):
+                multiply(acc[:], lw[:, s, :], ls[:, s, :], s)
+            res = opool.tile([P, 2 * LEFT], F32, tag="res", name="res")
+            nc.scalar.copy(out=res[:], in_=acc[:])
+            for b in range(NB):
+                nc.sync.dma_start(
+                    out=out_flat[b][:, q_of_b[b] : q_of_b[b] + LEFT],
+                    in_=res[:, b * LEFT : (b + 1) * LEFT],
+                )
+
+        work = []
+        q = 0
+        for n in GROUPS_B0:
+            work.append(("group", 0, q, n))
+            q += n
+        work.append(("left", 0, q, LEFT))
+        assert q + LEFT == NPX
+        work.append(("left", 1, 0, LEFT))
+        q = LEFT
+        for n in GROUPS_B1:
+            work.append(("group", 1, q, n))
+            q += n
+        assert q == NPX
+
+        def last_chunk_needed(b, q0, n):
+            top_row = (q0 + n - 1) // W + 2
+            return b * N_CH + min(N_CH - 1, max(0, (top_row - 1) // CH_ROWS))
+
+        def first_free_index(c):
+            if c < N_CH:
+                return 0
+            rb = (c - N_CH) * CH_ROWS + CH_ROWS
+            idx = 0
+            for i, (kind, b, q0, n) in enumerate(work):
+                if b == 0 and q0 // W <= rb:
+                    idx = i + 1
+            return idx
+
+        done = 0
+        for i, (kind, b, q0, n) in enumerate(work):
+            need = last_chunk_needed(b, q0, n)
+            while done < NB * N_CH and done <= need + LEAD and first_free_index(done) <= i:
+                prep_chunk(done // N_CH, done % N_CH, on_vector=(done == 0))
+                done += 1
+            assert done > need
+            if i == 0:
+                prep_weights()
+            if kind == "group":
+                group(b, q0, n)
+            else:
+                left_quantise(b, q0)
+                if b == 1:
+                    left_finish([NPX - LEFT, 0])

@@ -78,7 +78,7 @@ def tile_conv2d_kernel(tc, x, K, out):
                 nc.vector.tensor_copy(out=grow[2][:, ra:rb, 0:last], in_=grow[1][:, ra:rb, PACK:])
             else:
                 nc.scalar.copy(out=dst, in_=src)
-                nc.scalar.copy(out=grow[0][:, ra:rb, PACK:], in_=grow[1][:, ra:rb, 0:last])
+                nc.sync.dma_start(out=grow[0][:, ra:rb, PACK:], in_=grow[1][:, ra:rb, 0:last])
                 nc.scalar.copy(out=grow[2][:, ra:rb, 0:last], in_=grow[1][:, ra:rb, PACK:])
 
         kg = keep.tile([P, TAPS * C_OUT, PACK], BF16, align_bytes=64, name="kg")

@@ -60,6 +60,7 @@ def tile_conv2d_kernel(tc, x, K, out):
 
         g = [keep.tile([P, RP * W, PACK], BF16, align_bytes=64, name="g%d" % dj) for dj in range(3)]
         grow = [t[:].rearrange("p (r j) t -> p r (j t)", j=W) for t in g]
+        gword = [t[:].rearrange("p q t -> p (q t)").bitcast(F32).rearrange("p (r v) -> p r v", r=RP) for t in g]
         for dj in range(3):
             nc.vector.memset(grow[dj][:, 0:1, :], 0.0)
             nc.vector.memset(grow[dj][:, RP - 1 : RP, :], 0.0)
@@ -78,8 +79,8 @@ def tile_conv2d_kernel(tc, x, K, out):
                 nc.vector.tensor_copy(out=grow[2][:, ra:rb, 0:last], in_=grow[1][:, ra:rb, PACK:])
             else:
                 nc.scalar.copy(out=dst, in_=src)
-                nc.sync.dma_start(out=grow[0][:, ra:rb, PACK:], in_=grow[1][:, ra:rb, 0:last])
-                nc.scalar.copy(out=grow[2][:, ra:rb, 0:last], in_=grow[1][:, ra:rb, PACK:])
+                nc.scalar.copy(out=gword[0][:, ra:rb, 2:], in_=gword[1][:, ra:rb, 0 : last // 2])
+                nc.scalar.copy(out=gword[2][:, ra:rb, 0 : last // 2], in_=gword[1][:, ra:rb, 2:])
 
         kg = keep.tile([P, TAPS * C_OUT, PACK], BF16, align_bytes=64, name="kg")
         kw = keep.tile([P, TAPS * C_OUT], U32, align_bytes=64, name="kw")

@@ -19,12 +19,16 @@ NPX = H * W
 TAPS = 9
 CH_ROWS = 8
 N_CH = H // CH_ROWS
-LEAD = 1
+LEAD = 3
+LOADS_AHEAD = 4
+BANK = 512
 
 FLOPS = 2 * NB * NPX * 512 * TAPS * C_OUT
 
-GROUPS_B0 = [128, 256, 512, 512, 512, 512, 512, 128]
-GROUPS_B1 = [512, 512, 512, 512, 512, 256, 128, 128]
+TAP_ORDER = [1, 4, 7, 0, 3, 6, 2, 5, 8]
+HEAD = [128, 256]
+GROUPS_B0 = [512, 1024, 1024, 128]
+GROUPS_B1 = [1024, 1024, 512, 256, 128, 128]
 LEFT = 64
 
 
@@ -35,52 +39,58 @@ def tile_conv2d_kernel(tc, x, K, out):
         wpool = ctx.enter_context(tc.tile_pool(name="wpool", bufs=6))
         opool = ctx.enter_context(tc.tile_pool(name="opool", bufs=4))
         psum = ctx.enter_context(tc.psum_pool(name="psum", bufs=8))
+        ctx.enter_context(tc.manual_schedule())
 
         raw = {}
         kraw = keep.tile([P, PACK, TAPS * C_OUT], BF16, name="kraw")
 
-        def load_chunk(b, k):
-            t = keep.tile([P, PACK, CH_ROWS * W], BF16, name="raw%d_%d" % (b, k))
+        def load_chunk(c):
+            b, k = divmod(c, N_CH)
+            t = keep.tile([P, PACK, CH_ROWS * W], BF16, name="raw%d" % c)
             r0 = k * CH_ROWS
             nc.sync.dma_start(
                 out=t[:],
                 in_=x[b, :, r0 : r0 + CH_ROWS, :].rearrange("(p t) r c -> p t (r c)", t=PACK),
             )
-            raw[(b, k)] = t
+            raw[c] = t
 
-        load_chunk(0, 0)
+        load_chunk(0)
+        load_chunk(1)
         nc.sync.dma_start(
             out=kraw[:].rearrange("p t f -> p (t f)"),
             in_=K.rearrange("a b c o -> (a b c) o").rearrange("(p f) o -> p (f o)", p=P),
         )
-        for b in range(NB):
-            for k in range(N_CH):
-                if (b, k) != (0, 0):
-                    load_chunk(b, k)
+        for c in range(2, 2 + LOADS_AHEAD):
+            load_chunk(c)
 
         g = [keep.tile([P, RP * W, PACK], BF16, align_bytes=64, name="g%d" % dj) for dj in range(3)]
         grow = [t[:].rearrange("p (r j) t -> p r (j t)", j=W) for t in g]
         gword = [t[:].rearrange("p q t -> p (q t)").bitcast(F32).rearrange("p (r v) -> p r v", r=RP) for t in g]
-        for dj in range(3):
+        for dj in (1, 0, 2):
             nc.vector.memset(grow[dj][:, 0:1, :], 0.0)
             nc.vector.memset(grow[dj][:, RP - 1 : RP, :], 0.0)
         nc.vector.memset(grow[0][:, 1 : RP - 1, 0 : 4 * PACK], 0.0)
         nc.vector.memset(grow[2][:, 1 : RP - 1, (W - 4) * PACK : W * PACK], 0.0)
 
-        def prep_chunk(b, k, on_vector):
+        def prep_chunk(c):
+            k = c % N_CH
             ra = k * CH_ROWS + 1
             rb = ra + CH_ROWS
             dst = g[1][:, ra * W : rb * W, :].rearrange("p (c i) t -> p c t i", i=4)
-            src = raw[(b, k)][:].rearrange("p t (c i) -> p c t i", i=4)
+            src = raw[c][:].rearrange("p t (c i) -> p c t i", i=4)
             last = (W - 1) * PACK
-            if on_vector:
+            if c == 0:
                 nc.vector.tensor_copy(out=dst, in_=src)
-                nc.vector.tensor_copy(out=grow[0][:, ra:rb, PACK:], in_=grow[1][:, ra:rb, 0:last])
-                nc.vector.tensor_copy(out=grow[2][:, ra:rb, 0:last], in_=grow[1][:, ra:rb, PACK:])
             else:
                 nc.scalar.copy(out=dst, in_=src)
+            if c < 2:
                 nc.scalar.copy(out=gword[0][:, ra:rb, 2:], in_=gword[1][:, ra:rb, 0 : last // 2])
                 nc.scalar.copy(out=gword[2][:, ra:rb, 0 : last // 2], in_=gword[1][:, ra:rb, 2:])
+            else:
+                nc.sync.dma_start(out=grow[0][:, ra:rb, PACK:], in_=grow[1][:, ra:rb, 0:last])
+                nc.sync.dma_start(out=grow[2][:, ra:rb, 0:last], in_=grow[1][:, ra:rb, PACK:])
+                if c + LOADS_AHEAD < NB * N_CH:
+                    load_chunk(c + LOADS_AHEAD)
 
         kg = keep.tile([P, TAPS * C_OUT, PACK], BF16, align_bytes=64, name="kg")
         kw = keep.tile([P, TAPS * C_OUT], U32, align_bytes=64, name="kw")
@@ -107,51 +117,74 @@ def tile_conv2d_kernel(tc, x, K, out):
                 in_=g[dj][:, a : a + n, :].rearrange("p q t -> p (q t)"),
             )
 
-        def multiply(acc, src_w, src_s, s):
+        def multiply(acc, src_w, src_s, idx):
+            s = TAP_ORDER[idx]
             nc.tensor.matmul_mx(
                 out=acc,
                 lhsT=kw[:, s * C_OUT : (s + 1) * C_OUT].bitcast(FP8X4),
                 lhsT_scale=ks[:, s * C_OUT : (s + 1) * C_OUT],
                 rhs=src_w.bitcast(FP8X4),
                 rhs_scale=src_s,
-                start=(s == 0),
-                stop=(s == TAPS - 1),
+                start=(idx == 0),
+                stop=(idx == TAPS - 1),
             )
 
         out_flat = [out[b].rearrange("o i j -> o (i j)") for b in range(NB)]
 
-        def group(b, q0, n):
-            acc = psum.tile([P, n], F32, tag="acc", name="acc")
-            for s in range(TAPS):
-                w = wpool.tile([P, n], U32, align_bytes=64, tag="w", name="w")
-                sc = wpool.tile([P, n], U8, align_bytes=64, tag="sc", name="sc")
-                quantise(w[:], sc[:], s, q0, n)
-                multiply(acc[:], w[:], sc[:], s)
+        def finish(acc, n, pieces):
             res = opool.tile([P, n], F32, tag="res", name="res")
             nc.scalar.copy(out=res[:], in_=acc[:])
-            nc.sync.dma_start(out=out_flat[b][:, q0 : q0 + n], in_=res[:])
+            for b, q0, c0, m in pieces:
+                nc.sync.dma_start(out=out_flat[b][:, q0 : q0 + m], in_=res[:, c0 : c0 + m])
+
+        def group(b, q0, n):
+            width = min(n, BANK)
+            accs = [psum.tile([P, width], F32, tag="acc", name="acc%d" % h) for h in range(n // width)]
+            for idx in range(TAPS):
+                w = wpool.tile([P, n], U32, align_bytes=64, tag="w", name="w")
+                sc = wpool.tile([P, n], U8, align_bytes=64, tag="sc", name="sc")
+                quantise(w[:], sc[:], TAP_ORDER[idx], q0, n)
+                for h, acc in enumerate(accs):
+                    multiply(acc[:], w[:, h * width : (h + 1) * width], sc[:, h * width : (h + 1) * width], idx)
+            for h, acc in enumerate(accs):
+                finish(acc, width, [(b, q0 + h * width, 0, width)])
+
+        n_head = sum(HEAD)
+        hw = keep.tile([P, TAPS, n_head], U32, align_bytes=64, name="hw")
+        hs = keep.tile([P, TAPS, n_head], U8, align_bytes=64, name="hs")
+
+        def head():
+            for idx in range(TAPS):
+                c0 = 0
+                for n in HEAD:
+                    quantise(hw[:, idx, c0 : c0 + n], hs[:, idx, c0 : c0 + n], TAP_ORDER[idx], c0, n)
+                    c0 += n
+            prep_weights()
+            c0 = 0
+            for n in HEAD:
+                acc = psum.tile([P, n], F32, tag="acc", name="acch")
+                for idx in range(TAPS):
+                    multiply(acc[:], hw[:, idx, c0 : c0 + n], hs[:, idx, c0 : c0 + n], idx)
+                finish(acc, n, [(0, c0, 0, n)])
+                c0 += n
 
         lw = keep.tile([P, TAPS, 2 * LEFT], U32, align_bytes=64, name="lw")
         ls = keep.tile([P, TAPS, 2 * LEFT], U8, align_bytes=64, name="ls")
 
         def left_quantise(b, q0):
-            for s in range(TAPS):
-                quantise(lw[:, s, b * LEFT : (b + 1) * LEFT], ls[:, s, b * LEFT : (b + 1) * LEFT], s, q0, LEFT)
-
-        def left_finish(q_of_b):
-            acc = psum.tile([P, 2 * LEFT], F32, tag="acc", name="acc")
-            for s in range(TAPS):
-                multiply(acc[:], lw[:, s, :], ls[:, s, :], s)
-            res = opool.tile([P, 2 * LEFT], F32, tag="res", name="res")
-            nc.scalar.copy(out=res[:], in_=acc[:])
-            for b in range(NB):
-                nc.sync.dma_start(
-                    out=out_flat[b][:, q_of_b[b] : q_of_b[b] + LEFT],
-                    in_=res[:, b * LEFT : (b + 1) * LEFT],
+            for idx in range(TAPS):
+                quantise(
+                    lw[:, idx, b * LEFT : (b + 1) * LEFT], ls[:, idx, b * LEFT : (b + 1) * LEFT], TAP_ORDER[idx], q0, LEFT
                 )
 
-        work = []
-        q = 0
+        def left_finish(q_of_b):
+            acc = psum.tile([P, 2 * LEFT], F32, tag="acc", name="accl")
+            for idx in range(TAPS):
+                multiply(acc[:], lw[:, idx, :], ls[:, idx, :], idx)
+            finish(acc, 2 * LEFT, [(b, q_of_b[b], b * LEFT, LEFT) for b in range(NB)])
+
+        work = [("head", 0, 0, n_head)]
+        q = n_head
         for n in GROUPS_B0:
             work.append(("group", 0, q, n))
             q += n
@@ -182,12 +215,12 @@ def tile_conv2d_kernel(tc, x, K, out):
         for i, (kind, b, q0, n) in enumerate(work):
             need = last_chunk_needed(b, q0, n)
             while done < NB * N_CH and done <= need + LEAD and first_free_index(done) <= i:
-                prep_chunk(done // N_CH, done % N_CH, on_vector=(done == 0))
+                prep_chunk(done)
                 done += 1
             assert done > need
-            if i == 0:
-                prep_weights()
-            if kind == "group":
+            if kind == "head":
+                head()
+            elif kind == "group":
                 group(b, q0, n)
             else:
                 left_quantise(b, q0)

@@ -1,6 +1,7 @@
 from contextlib import ExitStack
 
 import concourse.mybir as mybir
+from concourse.masks import make_identity
 
 BF16 = mybir.dt.bfloat16
 F32 = mybir.dt.float32
@@ -18,27 +19,29 @@ RP = H + 2
 NPX = H * W
 TAPS = 9
 CH_ROWS = 8
+BLK_ROWS = 4
 N_CH = H // CH_ROWS
-LEAD = 3
-LOADS_AHEAD = 4
-BANK = 512
+LEAD = 2
+KBLK = 256
 
 FLOPS = 2 * NB * NPX * 512 * TAPS * C_OUT
 
 TAP_ORDER = [1, 4, 7, 0, 3, 6, 2, 5, 8]
-HEAD = [128, 256]
-GROUPS_B0 = [512, 1024, 1024, 128]
-GROUPS_B1 = [1024, 1024, 512, 256, 128, 128]
+HEAD = [128, 256, 256]
+GROUPS_B0 = [128, 512, 256, 512, 512, 512]
+GROUPS_B1 = [512, 512, 512, 512, 512, 256, 128, 128]
 LEFT = 64
+DIRECT_CHUNKS = (6, 8, 10, 12)
 
 
 def tile_conv2d_kernel(tc, x, K, out):
     nc = tc.nc
     with ExitStack() as ctx:
         keep = ctx.enter_context(tc.tile_pool(name="keep", bufs=1))
-        wpool = ctx.enter_context(tc.tile_pool(name="wpool", bufs=6))
+        wpool = ctx.enter_context(tc.tile_pool(name="wpool", bufs=8))
         opool = ctx.enter_context(tc.tile_pool(name="opool", bufs=4))
-        psum = ctx.enter_context(tc.psum_pool(name="psum", bufs=8))
+        psum = ctx.enter_context(tc.psum_pool(name="psum", bufs=5))
+        ipool = ctx.enter_context(tc.psum_pool(name="ipool", bufs=3))
         ctx.enter_context(tc.manual_schedule())
 
         raw = {}
@@ -60,8 +63,11 @@ def tile_conv2d_kernel(tc, x, K, out):
             out=kraw[:].rearrange("p t f -> p (t f)"),
             in_=K.rearrange("a b c o -> (a b c) o").rearrange("(p f) o -> p (f o)", p=P),
         )
-        for c in range(2, 2 + LOADS_AHEAD):
+        for c in range(2, NB * N_CH):
             load_chunk(c)
+
+        ident = keep.tile([P, P], BF16, name="ident")
+        make_identity(nc, ident[:])
 
         g = [keep.tile([P, RP * W, PACK], BF16, align_bytes=64, name="g%d" % dj) for dj in range(3)]
         grow = [t[:].rearrange("p (r j) t -> p r (j t)", j=W) for t in g]
@@ -72,35 +78,56 @@ def tile_conv2d_kernel(tc, x, K, out):
         nc.vector.memset(grow[0][:, 1 : RP - 1, 0 : 4 * PACK], 0.0)
         nc.vector.memset(grow[2][:, 1 : RP - 1, (W - 4) * PACK : W * PACK], 0.0)
 
+        last = (W - 1) * PACK
+
+        def interleave_on_tensor(planes, n):
+            ps = ipool.tile([P, KBLK, PACK], BF16, tag="ip", name="ip")
+            for v in range(2):
+                nc.tensor.matmul(
+                    out=ps[:, 0:n, 2 * v : 2 * v + 2],
+                    lhsT=ident[:],
+                    rhs=planes[:, 2 * v : 2 * v + 2, :].rearrange("p u c -> p c u"),
+                    start=True,
+                    stop=True,
+                )
+            return ps
+
         def prep_chunk(c):
-            k = c % N_CH
-            ra = k * CH_ROWS + 1
+            ra = (c % N_CH) * CH_ROWS + 1
             rb = ra + CH_ROWS
-            dst = g[1][:, ra * W : rb * W, :].rearrange("p (c i) t -> p c t i", i=4)
-            src = raw[c][:].rearrange("p t (c i) -> p c t i", i=4)
-            last = (W - 1) * PACK
-            if c == 0:
-                nc.vector.tensor_copy(out=dst, in_=src)
-            else:
-                nc.scalar.copy(out=dst, in_=src)
-            if c < 2:
-                nc.scalar.copy(out=gword[0][:, ra:rb, 2:], in_=gword[1][:, ra:rb, 0 : last // 2])
-                nc.scalar.copy(out=gword[2][:, ra:rb, 0 : last // 2], in_=gword[1][:, ra:rb, 2:])
-            else:
-                nc.sync.dma_start(out=grow[0][:, ra:rb, PACK:], in_=grow[1][:, ra:rb, 0:last])
-                nc.sync.dma_start(out=grow[2][:, ra:rb, 0:last], in_=grow[1][:, ra:rb, PACK:])
-                if c + LOADS_AHEAD < NB * N_CH:
-                    load_chunk(c + LOADS_AHEAD)
+            if c == 0 or c in DIRECT_CHUNKS:
+                dst = g[1][:, ra * W : rb * W, :].rearrange("p (c i) t -> p c t i", i=4)
+                src = raw[c][:].rearrange("p t (c i) -> p c t i", i=4)
+                if c == 0:
+                    nc.vector.tensor_copy(out=dst, in_=src)
+                    nc.vector.tensor_copy(out=grow[0][:, ra:rb, PACK:], in_=grow[1][:, ra:rb, 0:last])
+                    nc.vector.tensor_copy(out=grow[2][:, ra:rb, 0:last], in_=grow[1][:, ra:rb, PACK:])
+                else:
+                    nc.scalar.copy(out=dst, in_=src)
+                    nc.scalar.copy(out=gword[0][:, ra:rb, 2:], in_=gword[1][:, ra:rb, 0 : last // 2])
+                    nc.scalar.copy(out=gword[2][:, ra:rb, 0 : last // 2], in_=gword[1][:, ra:rb, 2:])
+                return
+            n = BLK_ROWS * W
+            for blk in range(CH_ROWS // BLK_ROWS):
+                r0 = ra + blk * BLK_ROWS
+                r1 = r0 + BLK_ROWS
+                ps = interleave_on_tensor(raw[c][:, :, blk * n : (blk + 1) * n], n)
+                psrow = ps[:, 0:n, :].rearrange("p (r j) t -> p r (j t)", j=W)
+                nc.scalar.copy(out=g[1][:, r0 * W : r1 * W, :], in_=ps[:, 0:n, :])
+                nc.scalar.copy(out=grow[0][:, r0:r1, PACK:], in_=psrow[:, :, 0:last])
+                nc.scalar.copy(out=grow[2][:, r0:r1, 0:last], in_=psrow[:, :, PACK:])
 
         kg = keep.tile([P, TAPS * C_OUT, PACK], BF16, align_bytes=64, name="kg")
         kw = keep.tile([P, TAPS * C_OUT], U32, align_bytes=64, name="kw")
         ks = keep.tile([P, TAPS * C_OUT], U8, align_bytes=64, name="ks")
 
-        def prep_weights():
-            nc.vector.tensor_copy(
-                out=kg[:].rearrange("p (c i) t -> p c t i", i=4),
-                in_=kraw[:].rearrange("p t (c i) -> p c t i", i=4),
-            )
+        def interleave_weights():
+            for c0 in range(0, TAPS * C_OUT, KBLK):
+                n = min(KBLK, TAPS * C_OUT - c0)
+                ps = interleave_on_tensor(kraw[:, :, c0 : c0 + n], n)
+                nc.scalar.copy(out=kg[:, c0 : c0 + n, :], in_=ps[:, 0:n, :])
+
+        def quantise_weights():
             for c0, c1 in ((0, 1024), (1024, 1152)):
                 nc.vector.quantize_mx(
                     out=kw[:, c0:c1].bitcast(FP8X4),
@@ -130,42 +157,44 @@ def tile_conv2d_kernel(tc, x, K, out):
             )
 
         out_flat = [out[b].rearrange("o i j -> o (i j)") for b in range(NB)]
+        pending = []
+        flushed = [0]
 
-        def finish(acc, n, pieces):
-            res = opool.tile([P, n], F32, tag="res", name="res")
-            nc.scalar.copy(out=res[:], in_=acc[:])
-            for b, q0, c0, m in pieces:
-                nc.sync.dma_start(out=out_flat[b][:, q0 : q0 + m], in_=res[:, c0 : c0 + m])
+        def flush(keep_last):
+            while len(pending) - flushed[0] > keep_last:
+                acc, n, pieces = pending[flushed[0]]
+                flushed[0] += 1
+                res = opool.tile([P, n], F32, tag="res", name="res")
+                nc.scalar.copy(out=res[:], in_=acc[:])
+                for b, q0, c0, m in pieces:
+                    nc.sync.dma_start(out=out_flat[b][:, q0 : q0 + m], in_=res[:, c0 : c0 + m])
 
         def group(b, q0, n):
-            width = min(n, BANK)
-            accs = [psum.tile([P, width], F32, tag="acc", name="acc%d" % h) for h in range(n // width)]
+            acc = psum.tile([P, n], F32, tag="acc", name="acc")
             for idx in range(TAPS):
                 w = wpool.tile([P, n], U32, align_bytes=64, tag="w", name="w")
                 sc = wpool.tile([P, n], U8, align_bytes=64, tag="sc", name="sc")
                 quantise(w[:], sc[:], TAP_ORDER[idx], q0, n)
-                for h, acc in enumerate(accs):
-                    multiply(acc[:], w[:, h * width : (h + 1) * width], sc[:, h * width : (h + 1) * width], idx)
-            for h, acc in enumerate(accs):
-                finish(acc, width, [(b, q0 + h * width, 0, width)])
+                multiply(acc[:], w[:], sc[:], idx)
+            pending.append((acc, n, [(b, q0, 0, n)]))
 
         n_head = sum(HEAD)
         hw = keep.tile([P, TAPS, n_head], U32, align_bytes=64, name="hw")
         hs = keep.tile([P, TAPS, n_head], U8, align_bytes=64, name="hs")
 
         def head():
-            for idx in range(TAPS):
-                c0 = 0
-                for n in HEAD:
+            c0 = 0
+            for n in HEAD:
+                for idx in range(TAPS):
                     quantise(hw[:, idx, c0 : c0 + n], hs[:, idx, c0 : c0 + n], TAP_ORDER[idx], c0, n)
-                    c0 += n
-            prep_weights()
+                c0 += n
+            quantise_weights()
             c0 = 0
             for n in HEAD:
                 acc = psum.tile([P, n], F32, tag="acc", name="acch")
                 for idx in range(TAPS):
                     multiply(acc[:], hw[:, idx, c0 : c0 + n], hs[:, idx, c0 : c0 + n], idx)
-                finish(acc, n, [(0, c0, 0, n)])
+                pending.append((acc, n, [(0, c0, 0, n)]))
                 c0 += n
 
         lw = keep.tile([P, TAPS, 2 * LEFT], U32, align_bytes=64, name="lw")
@@ -181,7 +210,7 @@ def tile_conv2d_kernel(tc, x, K, out):
             acc = psum.tile([P, 2 * LEFT], F32, tag="acc", name="accl")
             for idx in range(TAPS):
                 multiply(acc[:], lw[:, idx, :], ls[:, idx, :], idx)
-            finish(acc, 2 * LEFT, [(b, q_of_b[b], b * LEFT, LEFT) for b in range(NB)])
+            pending.append((acc, 2 * LEFT, [(b, q_of_b[b], b * LEFT, LEFT) for b in range(NB)]))
 
         work = [("head", 0, 0, n_head)]
         q = n_head
@@ -217,6 +246,8 @@ def tile_conv2d_kernel(tc, x, K, out):
             while done < NB * N_CH and done <= need + LEAD and first_free_index(done) <= i:
                 prep_chunk(done)
                 done += 1
+                if done == 2:
+                    interleave_weights()
             assert done > need
             if kind == "head":
                 head()
@@ -226,3 +257,5 @@ def tile_conv2d_kernel(tc, x, K, out):
                 left_quantise(b, q0)
                 if b == 1:
                     left_finish([NPX - LEFT, 0])
+            flush(1)
+        flush(0)

@@ -1,7 +1,6 @@
 from contextlib import ExitStack
 
 import concourse.mybir as mybir
-from concourse.masks import make_identity
 
 BF16 = mybir.dt.bfloat16
 F32 = mybir.dt.float32
@@ -19,30 +18,26 @@ RP = H + 2
 NPX = H * W
 TAPS = 9
 CH_ROWS = 8
-BLK_ROWS = 4
 N_CH = H // CH_ROWS
-LEAD = 2
-KBLK = 256
+LEAD = 1
+BANK = 512
 
 FLOPS = 2 * NB * NPX * 512 * TAPS * C_OUT
 
-TAP_ORDER = [1, 4, 7, 0, 3, 6, 2, 5, 8]
-HEAD = [128, 256, 256]
-GROUPS_B0 = [128, 512, 256, 512, 512, 512]
-GROUPS_B1 = [512, 512, 512, 512, 512, 256, 128, 128]
+TAP_ORDER = [0, 1, 2, 3, 4, 5, 6, 7, 8]
+HEAD = [128, 256]
+GROUPS_B0 = [512, 512, 512, 1024, 128]
+GROUPS_B1 = [1024, 1024, 512, 256, 128, 128]
 LEFT = 64
-DIRECT_CHUNKS = (6, 8, 10, 12)
 
 
 def tile_conv2d_kernel(tc, x, K, out):
     nc = tc.nc
     with ExitStack() as ctx:
         keep = ctx.enter_context(tc.tile_pool(name="keep", bufs=1))
-        wpool = ctx.enter_context(tc.tile_pool(name="wpool", bufs=8))
+        wpool = ctx.enter_context(tc.tile_pool(name="wpool", bufs=6))
         opool = ctx.enter_context(tc.tile_pool(name="opool", bufs=4))
-        psum = ctx.enter_context(tc.psum_pool(name="psum", bufs=5))
-        ipool = ctx.enter_context(tc.psum_pool(name="ipool", bufs=3))
-        ctx.enter_context(tc.manual_schedule())
+        psum = ctx.enter_context(tc.psum_pool(name="psum", bufs=8))
 
         raw = {}
         kraw = keep.tile([P, PACK, TAPS * C_OUT], BF16, name="kraw")
@@ -66,9 +61,6 @@ def tile_conv2d_kernel(tc, x, K, out):
         for c in range(2, NB * N_CH):
             load_chunk(c)
 
-        ident = keep.tile([P, P], BF16, name="ident")
-        make_identity(nc, ident[:])
-
         g = [keep.tile([P, RP * W, PACK], BF16, align_bytes=64, name="g%d" % dj) for dj in range(3)]
         grow = [t[:].rearrange("p (r j) t -> p r (j t)", j=W) for t in g]
         gword = [t[:].rearrange("p q t -> p (q t)").bitcast(F32).rearrange("p (r v) -> p r v", r=RP) for t in g]
@@ -78,56 +70,31 @@ def tile_conv2d_kernel(tc, x, K, out):
         nc.vector.memset(grow[0][:, 1 : RP - 1, 0 : 4 * PACK], 0.0)
         nc.vector.memset(grow[2][:, 1 : RP - 1, (W - 4) * PACK : W * PACK], 0.0)
 
-        last = (W - 1) * PACK
-
-        def interleave_on_tensor(planes, n):
-            ps = ipool.tile([P, KBLK, PACK], BF16, tag="ip", name="ip")
-            for v in range(2):
-                nc.tensor.matmul(
-                    out=ps[:, 0:n, 2 * v : 2 * v + 2],
-                    lhsT=ident[:],
-                    rhs=planes[:, 2 * v : 2 * v + 2, :].rearrange("p u c -> p c u"),
-                    start=True,
-                    stop=True,
-                )
-            return ps
-
         def prep_chunk(c):
-            ra = (c % N_CH) * CH_ROWS + 1
+            k = c % N_CH
+            ra = k * CH_ROWS + 1
             rb = ra + CH_ROWS
-            if c == 0 or c in DIRECT_CHUNKS:
-                dst = g[1][:, ra * W : rb * W, :].rearrange("p (c i) t -> p c t i", i=4)
-                src = raw[c][:].rearrange("p t (c i) -> p c t i", i=4)
-                if c == 0:
-                    nc.vector.tensor_copy(out=dst, in_=src)
-                    nc.vector.tensor_copy(out=grow[0][:, ra:rb, PACK:], in_=grow[1][:, ra:rb, 0:last])
-                    nc.vector.tensor_copy(out=grow[2][:, ra:rb, 0:last], in_=grow[1][:, ra:rb, PACK:])
-                else:
-                    nc.scalar.copy(out=dst, in_=src)
-                    nc.scalar.copy(out=gword[0][:, ra:rb, 2:], in_=gword[1][:, ra:rb, 0 : last // 2])
-                    nc.scalar.copy(out=gword[2][:, ra:rb, 0 : last // 2], in_=gword[1][:, ra:rb, 2:])
-                return
-            n = BLK_ROWS * W
-            for blk in range(CH_ROWS // BLK_ROWS):
-                r0 = ra + blk * BLK_ROWS
-                r1 = r0 + BLK_ROWS
-                ps = interleave_on_tensor(raw[c][:, :, blk * n : (blk + 1) * n], n)
-                psrow = ps[:, 0:n, :].rearrange("p (r j) t -> p r (j t)", j=W)
-                nc.scalar.copy(out=g[1][:, r0 * W : r1 * W, :], in_=ps[:, 0:n, :])
-                nc.scalar.copy(out=grow[0][:, r0:r1, PACK:], in_=psrow[:, :, 0:last])
-                nc.scalar.copy(out=grow[2][:, r0:r1, 0:last], in_=psrow[:, :, PACK:])
+            dst = g[1][:, ra * W : rb * W, :].rearrange("p (c i) t -> p c t i", i=4)
+            src = raw[c][:].rearrange("p t (c i) -> p c t i", i=4)
+            last = (W - 1) * PACK
+            if c == 0:
+                nc.vector.tensor_copy(out=dst, in_=src)
+                nc.vector.tensor_copy(out=grow[0][:, ra:rb, PACK:], in_=grow[1][:, ra:rb, 0:last])
+                nc.vector.tensor_copy(out=grow[2][:, ra:rb, 0:last], in_=grow[1][:, ra:rb, PACK:])
+            else:
+                nc.scalar.copy(out=dst, in_=src)
+                nc.scalar.copy(out=gword[0][:, ra:rb, 2:], in_=gword[1][:, ra:rb, 0 : last // 2])
+                nc.scalar.copy(out=gword[2][:, ra:rb, 0 : last // 2], in_=gword[1][:, ra:rb, 2:])
 
         kg = keep.tile([P, TAPS * C_OUT, PACK], BF16, align_bytes=64, name="kg")
         kw = keep.tile([P, TAPS * C_OUT], U32, align_bytes=64, name="kw")
         ks = keep.tile([P, TAPS * C_OUT], U8, align_bytes=64, name="ks")
 
-        def interleave_weights():
-            for c0 in range(0, TAPS * C_OUT, KBLK):
-                n = min(KBLK, TAPS * C_OUT - c0)
-                ps = interleave_on_tensor(kraw[:, :, c0 : c0 + n], n)
-                nc.scalar.copy(out=kg[:, c0 : c0 + n, :], in_=ps[:, 0:n, :])
-
-        def quantise_weights():
+        def prep_weights():
+            nc.vector.tensor_copy(
+                out=kg[:].rearrange("p (c i) t -> p c t i", i=4),
+                in_=kraw[:].rearrange("p t (c i) -> p c t i", i=4),
+            )
             for c0, c1 in ((0, 1024), (1024, 1152)):
                 nc.vector.quantize_mx(
                     out=kw[:, c0:c1].bitcast(FP8X4),
@@ -157,44 +124,42 @@ def tile_conv2d_kernel(tc, x, K, out):
             )
 
         out_flat = [out[b].rearrange("o i j -> o (i j)") for b in range(NB)]
-        pending = []
-        flushed = [0]
 
-        def flush(keep_last):
-            while len(pending) - flushed[0] > keep_last:
-                acc, n, pieces = pending[flushed[0]]
-                flushed[0] += 1
-                res = opool.tile([P, n], F32, tag="res", name="res")
-                nc.scalar.copy(out=res[:], in_=acc[:])
-                for b, q0, c0, m in pieces:
-                    nc.sync.dma_start(out=out_flat[b][:, q0 : q0 + m], in_=res[:, c0 : c0 + m])
+        def finish(acc, n, pieces):
+            res = opool.tile([P, n], F32, tag="res", name="res")
+            nc.scalar.copy(out=res[:], in_=acc[:])
+            for b, q0, c0, m in pieces:
+                nc.sync.dma_start(out=out_flat[b][:, q0 : q0 + m], in_=res[:, c0 : c0 + m])
 
         def group(b, q0, n):
-            acc = psum.tile([P, n], F32, tag="acc", name="acc")
+            width = min(n, BANK)
+            accs = [psum.tile([P, width], F32, tag="acc", name="acc%d" % h) for h in range(n // width)]
             for idx in range(TAPS):
                 w = wpool.tile([P, n], U32, align_bytes=64, tag="w", name="w")
                 sc = wpool.tile([P, n], U8, align_bytes=64, tag="sc", name="sc")
                 quantise(w[:], sc[:], TAP_ORDER[idx], q0, n)
-                multiply(acc[:], w[:], sc[:], idx)
-            pending.append((acc, n, [(b, q0, 0, n)]))
+                for h, acc in enumerate(accs):
+                    multiply(acc[:], w[:, h * width : (h + 1) * width], sc[:, h * width : (h + 1) * width], idx)
+            for h, acc in enumerate(accs):
+                finish(acc, width, [(b, q0 + h * width, 0, width)])
 
         n_head = sum(HEAD)
         hw = keep.tile([P, TAPS, n_head], U32, align_bytes=64, name="hw")
         hs = keep.tile([P, TAPS, n_head], U8, align_bytes=64, name="hs")
 
         def head():
-            c0 = 0
-            for n in HEAD:
-                for idx in range(TAPS):
+            for idx in range(TAPS):
+                c0 = 0
+                for n in HEAD:
                     quantise(hw[:, idx, c0 : c0 + n], hs[:, idx, c0 : c0 + n], TAP_ORDER[idx], c0, n)
-                c0 += n
-            quantise_weights()
+                    c0 += n
+            prep_weights()
             c0 = 0
             for n in HEAD:
                 acc = psum.tile([P, n], F32, tag="acc", name="acch")
                 for idx in range(TAPS):
                     multiply(acc[:], hw[:, idx, c0 : c0 + n], hs[:, idx, c0 : c0 + n], idx)
-                pending.append((acc, n, [(0, c0, 0, n)]))
+                finish(acc, n, [(0, c0, 0, n)])
                 c0 += n
 
         lw = keep.tile([P, TAPS, 2 * LEFT], U32, align_bytes=64, name="lw")
@@ -210,7 +175,7 @@ def tile_conv2d_kernel(tc, x, K, out):
             acc = psum.tile([P, 2 * LEFT], F32, tag="acc", name="accl")
             for idx in range(TAPS):
                 multiply(acc[:], lw[:, idx, :], ls[:, idx, :], idx)
-            pending.append((acc, 2 * LEFT, [(b, q_of_b[b], b * LEFT, LEFT) for b in range(NB)]))
+            finish(acc, 2 * LEFT, [(b, q_of_b[b], b * LEFT, LEFT) for b in range(NB)])
 
         work = [("head", 0, 0, n_head)]
         q = n_head
@@ -246,8 +211,6 @@ def tile_conv2d_kernel(tc, x, K, out):
             while done < NB * N_CH and done <= need + LEAD and first_free_index(done) <= i:
                 prep_chunk(done)
                 done += 1
-                if done == 2:
-                    interleave_weights()
             assert done > need
             if kind == "head":
                 head()
@@ -257,5 +220,3 @@ def tile_conv2d_kernel(tc, x, K, out):
                 left_quantise(b, q0)
                 if b == 1:
                     left_finish([NPX - LEFT, 0])
-            flush(1)
-        flush(0)

@@ -19,7 +19,8 @@ NPX = H * W
 TAPS = 9
 CH_ROWS = 8
 N_CH = H // CH_ROWS
-LEAD = 1
+LEAD = 3
+KEEP_BANKS = 4
 BANK = 512
 
 FLOPS = 2 * NB * NPX * 512 * TAPS * C_OUT
@@ -38,6 +39,7 @@ def tile_conv2d_kernel(tc, x, K, out):
         wpool = ctx.enter_context(tc.tile_pool(name="wpool", bufs=6))
         opool = ctx.enter_context(tc.tile_pool(name="opool", bufs=4))
         psum = ctx.enter_context(tc.psum_pool(name="psum", bufs=8))
+        ctx.enter_context(tc.manual_schedule())
 
         raw = {}
         kraw = keep.tile([P, PACK, TAPS * C_OUT], BF16, name="kraw")
@@ -125,11 +127,20 @@ def tile_conv2d_kernel(tc, x, K, out):
 
         out_flat = [out[b].rearrange("o i j -> o (i j)") for b in range(NB)]
 
+        pending = []
+        flushed = [0]
+
         def finish(acc, n, pieces):
-            res = opool.tile([P, n], F32, tag="res", name="res")
-            nc.scalar.copy(out=res[:], in_=acc[:])
-            for b, q0, c0, m in pieces:
-                nc.sync.dma_start(out=out_flat[b][:, q0 : q0 + m], in_=res[:, c0 : c0 + m])
+            pending.append((acc, n, pieces))
+
+        def flush(keep_last):
+            while len(pending) - flushed[0] > keep_last:
+                acc, n, pieces = pending[flushed[0]]
+                flushed[0] += 1
+                res = opool.tile([P, n], F32, tag="res", name="res")
+                nc.scalar.copy(out=res[:], in_=acc[:])
+                for b, q0, c0, m in pieces:
+                    nc.sync.dma_start(out=out_flat[b][:, q0 : q0 + m], in_=res[:, c0 : c0 + m])
 
         def group(b, q0, n):
             width = min(n, BANK)
@@ -220,3 +231,5 @@ def tile_conv2d_kernel(tc, x, K, out):
                 left_quantise(b, q0)
                 if b == 1:
                     left_finish([NPX - LEFT, 0])
+            flush(KEEP_BANKS)
+        flush(0)

@@ -25,10 +25,12 @@ BANK = 512
 
 FLOPS = 2 * NB * NPX * 512 * TAPS * C_OUT
 
-TAP_ORDER = [0, 1, 2, 3, 4, 5, 6, 7, 8]
-HEAD = [128, 256]
-GROUPS_B0 = [512, 512, 512, 1024, 128]
-GROUPS_B1 = [1024, 1024, 512, 256, 128, 128]
+TAP_ORDER = [1, 4, 7, 0, 3, 6, 2, 5, 8]
+HEAD = [256, 256]
+GROUPS_B0 = [512, 1024, 1024]
+GROUPS_B1 = [1024, 1024]
+LAST = 1024
+LAST_PIECE = 256
 LEFT = 64
 
 
@@ -56,11 +58,12 @@ def tile_conv2d_kernel(tc, x, K, out):
 
         load_chunk(0)
         load_chunk(1)
+        load_chunk(2)
         nc.sync.dma_start(
             out=kraw[:].rearrange("p t f -> p (t f)"),
             in_=K.rearrange("a b c o -> (a b c) o").rearrange("(p f) o -> p (f o)", p=P),
         )
-        for c in range(2, NB * N_CH):
+        for c in range(3, NB * N_CH):
             load_chunk(c)
 
         g = [keep.tile([P, RP * W, PACK], BF16, align_bytes=64, name="g%d" % dj) for dj in range(3)]
@@ -69,8 +72,8 @@ def tile_conv2d_kernel(tc, x, K, out):
         for dj in (1, 0, 2):
             nc.vector.memset(grow[dj][:, 0:1, :], 0.0)
             nc.vector.memset(grow[dj][:, RP - 1 : RP, :], 0.0)
-        nc.vector.memset(grow[0][:, 1 : RP - 1, 0 : 4 * PACK], 0.0)
-        nc.vector.memset(grow[2][:, 1 : RP - 1, (W - 4) * PACK : W * PACK], 0.0)
+        nc.gpsimd.memset(grow[0][:, 1 : RP - 1, 0:PACK], 0.0)
+        nc.gpsimd.memset(grow[2][:, 1 : RP - 1, (W - 1) * PACK : W * PACK], 0.0)
 
         def prep_chunk(c):
             k = c % N_CH
@@ -81,12 +84,10 @@ def tile_conv2d_kernel(tc, x, K, out):
             last = (W - 1) * PACK
             if c == 0:
                 nc.vector.tensor_copy(out=dst, in_=src)
-                nc.vector.tensor_copy(out=grow[0][:, ra:rb, PACK:], in_=grow[1][:, ra:rb, 0:last])
-                nc.vector.tensor_copy(out=grow[2][:, ra:rb, 0:last], in_=grow[1][:, ra:rb, PACK:])
             else:
                 nc.scalar.copy(out=dst, in_=src)
-                nc.scalar.copy(out=gword[0][:, ra:rb, 2:], in_=gword[1][:, ra:rb, 0 : last // 2])
-                nc.scalar.copy(out=gword[2][:, ra:rb, 0 : last // 2], in_=gword[1][:, ra:rb, 2:])
+            nc.scalar.copy(out=gword[0][:, ra:rb, 2:], in_=gword[1][:, ra:rb, 0 : last // 2])
+            nc.scalar.copy(out=gword[2][:, ra:rb, 0 : last // 2], in_=gword[1][:, ra:rb, 2:])
 
         kg = keep.tile([P, TAPS * C_OUT, PACK], BF16, align_bytes=64, name="kg")
         kw = keep.tile([P, TAPS * C_OUT], U32, align_bytes=64, name="kw")
@@ -154,53 +155,71 @@ def tile_conv2d_kernel(tc, x, K, out):
             for h, acc in enumerate(accs):
                 finish(acc, width, [(b, q0 + h * width, 0, width)])
 
+        def last_group(b, q0):
+            accs = [psum.tile([P, LAST_PIECE], F32, tag="acc", name="accz%d" % h) for h in range(LAST // LAST_PIECE)]
+            for idx in range(TAPS):
+                w = wpool.tile([P, LAST], U32, align_bytes=64, tag="w", name="w")
+                sc = wpool.tile([P, LAST], U8, align_bytes=64, tag="sc", name="sc")
+                if idx < TAPS - 1:
+                    quantise(w[:], sc[:], TAP_ORDER[idx], q0, LAST)
+                for h, acc in enumerate(accs):
+                    c0, c1 = h * LAST_PIECE, (h + 1) * LAST_PIECE
+                    if idx == TAPS - 1:
+                        quantise(w[:, c0:c1], sc[:, c0:c1], TAP_ORDER[idx], q0 + c0, LAST_PIECE)
+                    multiply(acc[:], w[:, c0:c1], sc[:, c0:c1], idx)
+            for h, acc in enumerate(accs):
+                finish(acc, LAST_PIECE, [(b, q0 + h * LAST_PIECE, 0, LAST_PIECE)])
+
         n_head = sum(HEAD)
         hw = keep.tile([P, TAPS, n_head], U32, align_bytes=64, name="hw")
         hs = keep.tile([P, TAPS, n_head], U8, align_bytes=64, name="hs")
 
-        def head():
+        def head_quantise(c0, n):
+            quantise_at = LEFT + c0
             for idx in range(TAPS):
-                c0 = 0
-                for n in HEAD:
-                    quantise(hw[:, idx, c0 : c0 + n], hs[:, idx, c0 : c0 + n], TAP_ORDER[idx], c0, n)
-                    c0 += n
-            prep_weights()
+                if c0 == 0:
+                    left_quantise(0, 0, idx)
+                quantise(hw[:, idx, c0 : c0 + n], hs[:, idx, c0 : c0 + n], TAP_ORDER[idx], quantise_at, n)
+
+        def head_multiply():
             c0 = 0
             for n in HEAD:
                 acc = psum.tile([P, n], F32, tag="acc", name="acch")
                 for idx in range(TAPS):
                     multiply(acc[:], hw[:, idx, c0 : c0 + n], hs[:, idx, c0 : c0 + n], idx)
-                finish(acc, n, [(0, c0, 0, n)])
+                finish(acc, n, [(0, LEFT + c0, 0, n)])
                 c0 += n
 
         lw = keep.tile([P, TAPS, 2 * LEFT], U32, align_bytes=64, name="lw")
         ls = keep.tile([P, TAPS, 2 * LEFT], U8, align_bytes=64, name="ls")
 
-        def left_quantise(b, q0):
-            for idx in range(TAPS):
-                quantise(
-                    lw[:, idx, b * LEFT : (b + 1) * LEFT], ls[:, idx, b * LEFT : (b + 1) * LEFT], TAP_ORDER[idx], q0, LEFT
-                )
+        def left_quantise(b, q0, idx):
+            quantise(
+                lw[:, idx, b * LEFT : (b + 1) * LEFT], ls[:, idx, b * LEFT : (b + 1) * LEFT], TAP_ORDER[idx], q0, LEFT
+            )
 
-        def left_finish(q_of_b):
+        def left_finish():
             acc = psum.tile([P, 2 * LEFT], F32, tag="acc", name="accl")
             for idx in range(TAPS):
                 multiply(acc[:], lw[:, idx, :], ls[:, idx, :], idx)
-            finish(acc, 2 * LEFT, [(b, q_of_b[b], b * LEFT, LEFT) for b in range(NB)])
+            finish(acc, 2 * LEFT, [(b, 0, b * LEFT, LEFT) for b in range(NB)])
 
-        work = [("head", 0, 0, n_head)]
-        q = n_head
+        work = []
+        q = LEFT
+        for n in HEAD:
+            work.append(("head", 0, q, n))
+            q += n
         for n in GROUPS_B0:
             work.append(("group", 0, q, n))
             q += n
-        work.append(("left", 0, q, LEFT))
-        assert q + LEFT == NPX
+        assert q == NPX
         work.append(("left", 1, 0, LEFT))
         q = LEFT
         for n in GROUPS_B1:
             work.append(("group", 1, q, n))
             q += n
-        assert q == NPX
+        work.append(("last", 1, q, LAST))
+        assert q + LAST == NPX
 
         def last_chunk_needed(b, q0, n):
             top_row = (q0 + n - 1) // W + 2
@@ -224,12 +243,17 @@ def tile_conv2d_kernel(tc, x, K, out):
                 done += 1
             assert done > need
             if kind == "head":
-                head()
+                head_quantise(q0 - LEFT, n)
+                if i == len(HEAD) - 1:
+                    prep_weights()
+                    head_multiply()
             elif kind == "group":
                 group(b, q0, n)
+            elif kind == "left":
+                for idx in range(TAPS):
+                    left_quantise(b, q0, idx)
+                left_finish()
             else:
-                left_quantise(b, q0)
-                if b == 1:
-                    left_finish([NPX - LEFT, 0])
+                last_group(b, q0)
             flush(KEEP_BANKS)
         flush(0)

@@ -26,8 +26,8 @@ BANK = 512
 FLOPS = 2 * NB * NPX * 512 * TAPS * C_OUT
 
 TAP_ORDER = [1, 4, 7, 0, 3, 6, 2, 5, 8]
-HEAD = [256, 256]
-GROUPS_B0 = [512, 1024, 1024]
+HEAD = [256]
+GROUPS_B0 = [256, 512, 1024, 1024]
 GROUPS_B1 = [1024, 1024]
 LAST = 1024
 LAST_PIECE = 256
@@ -38,7 +38,7 @@ def tile_conv2d_kernel(tc, x, K, out):
     nc = tc.nc
     with ExitStack() as ctx:
         keep = ctx.enter_context(tc.tile_pool(name="keep", bufs=1))
-        wpool = ctx.enter_context(tc.tile_pool(name="wpool", bufs=6))
+        wpool = ctx.enter_context(tc.tile_pool(name="wpool", bufs=8))
         opool = ctx.enter_context(tc.tile_pool(name="opool", bufs=4))
         psum = ctx.enter_context(tc.psum_pool(name="psum", bufs=8))
         ctx.enter_context(tc.manual_schedule())
@@ -58,12 +58,11 @@ def tile_conv2d_kernel(tc, x, K, out):
 
         load_chunk(0)
         load_chunk(1)
-        load_chunk(2)
         nc.sync.dma_start(
             out=kraw[:].rearrange("p t f -> p (t f)"),
             in_=K.rearrange("a b c o -> (a b c) o").rearrange("(p f) o -> p (f o)", p=P),
         )
-        for c in range(3, NB * N_CH):
+        for c in range(2, NB * N_CH):
             load_chunk(c)
 
         g = [keep.tile([P, RP * W, PACK], BF16, align_bytes=64, name="g%d" % dj) for dj in range(3)]

@@ -17,9 +17,12 @@ W = 56
 RP = H + 2
 NPX = H * W
 TAPS = 9
-CH_ROWS = 8
-N_CH = H // CH_ROWS
-LEAD = 3
+ROWS_B0 = [8, 8, 8, 16, 16]
+ROWS_B1 = [8, 16, 16, 16]
+CHUNKS = [
+    (b, sum(rows[:i]), sum(rows[: i + 1])) for b, rows in enumerate((ROWS_B0, ROWS_B1)) for i in range(len(rows))
+]
+LEAD_ROWS = 24
 KEEP_BANKS = 4
 BANK = 512
 
@@ -47,12 +50,11 @@ def tile_conv2d_kernel(tc, x, K, out):
         kraw = keep.tile([P, PACK, TAPS * C_OUT], BF16, name="kraw")
 
         def load_chunk(c):
-            b, k = divmod(c, N_CH)
-            t = keep.tile([P, PACK, CH_ROWS * W], BF16, name="raw%d" % c)
-            r0 = k * CH_ROWS
+            b, r0, r1 = CHUNKS[c]
+            t = keep.tile([P, PACK, (r1 - r0) * W], BF16, name="raw%d" % c)
             nc.sync.dma_start(
                 out=t[:],
-                in_=x[b, :, r0 : r0 + CH_ROWS, :].rearrange("(p t) r c -> p t (r c)", t=PACK),
+                in_=x[b, :, r0:r1, :].rearrange("(p t) r c -> p t (r c)", t=PACK),
             )
             raw[c] = t
 
@@ -62,7 +64,7 @@ def tile_conv2d_kernel(tc, x, K, out):
             out=kraw[:].rearrange("p t f -> p (t f)"),
             in_=K.rearrange("a b c o -> (a b c) o").rearrange("(p f) o -> p (f o)", p=P),
         )
-        for c in range(2, NB * N_CH):
+        for c in range(2, len(CHUNKS)):
             load_chunk(c)
 
         g = [keep.tile([P, RP * W, PACK], BF16, align_bytes=64, name="g%d" % dj) for dj in range(3)]
@@ -75,9 +77,8 @@ def tile_conv2d_kernel(tc, x, K, out):
         nc.gpsimd.memset(grow[2][:, 1 : RP - 1, (W - 1) * PACK : W * PACK], 0.0)
 
         def prep_chunk(c):
-            k = c % N_CH
-            ra = k * CH_ROWS + 1
-            rb = ra + CH_ROWS
+            b, r0, r1 = CHUNKS[c]
+            ra, rb = r0 + 1, r1 + 1
             dst = g[1][:, ra * W : rb * W, :].rearrange("p (c i) t -> p c t i", i=4)
             src = raw[c][:].rearrange("p t (c i) -> p c t i", i=4)
             last = (W - 1) * PACK
@@ -220,24 +221,32 @@ def tile_conv2d_kernel(tc, x, K, out):
         work.append(("last", 1, q, LAST))
         assert q + LAST == NPX
 
-        def last_chunk_needed(b, q0, n):
-            top_row = (q0 + n - 1) // W + 2
-            return b * N_CH + min(N_CH - 1, max(0, (top_row - 1) // CH_ROWS))
+        def chunk_of_row(b, row):
+            for c, (cb, r0, r1) in enumerate(CHUNKS):
+                if (cb, r1) > (b, row):
+                    return c
+            return len(CHUNKS) - 1
+
+        def last_row_needed(q0, n):
+            return min(H - 1, (q0 + n - 1) // W + 1)
 
         def first_free_index(c):
-            if c < N_CH:
-                return 0
-            rb = (c - N_CH) * CH_ROWS + CH_ROWS
+            cb, r0, r1 = CHUNKS[c]
             idx = 0
             for i, (kind, b, q0, n) in enumerate(work):
-                if b == 0 and q0 // W <= rb:
+                if cb == 1 and b == 0 and q0 // W <= r1:
                     idx = i + 1
             return idx
 
+        def ahead(b, row):
+            b, row = b + (row + LEAD_ROWS) // H, (row + LEAD_ROWS) % H
+            return chunk_of_row(b, row) if b < NB else len(CHUNKS) - 1
+
         done = 0
         for i, (kind, b, q0, n) in enumerate(work):
-            need = last_chunk_needed(b, q0, n)
-            while done < NB * N_CH and done <= need + LEAD and first_free_index(done) <= i:
+            row = last_row_needed(q0, n)
+            need = chunk_of_row(b, row)
+            while done <= ahead(b, row) and done < len(CHUNKS) and first_free_index(done) <= i:
                 prep_chunk(done)
                 done += 1
             assert done > need

@@ -30,18 +30,20 @@ FLOPS = 2 * NB * NPX * 512 * TAPS * C_OUT
 
 TAP_ORDER = [1, 4, 7, 0, 3, 6, 2, 5, 8]
 HEAD = [256]
-GROUPS_B0 = [256, 512, 1024, 1024]
+GROUPS_B0 = [512, 256, 1024, 1024]
 GROUPS_B1 = [1024, 1024]
 LAST = 1024
 LAST_PIECE = 256
+WARM_UP = 3
 LEFT = 64
+CENTRE_TAPS = 3
 
 
 def tile_conv2d_kernel(tc, x, K, out):
     nc = tc.nc
     with ExitStack() as ctx:
         keep = ctx.enter_context(tc.tile_pool(name="keep", bufs=1))
-        wpool = ctx.enter_context(tc.tile_pool(name="wpool", bufs=8))
+        wpool = ctx.enter_context(tc.tile_pool(name="wpool", bufs=10))
         opool = ctx.enter_context(tc.tile_pool(name="opool", bufs=4))
         psum = ctx.enter_context(tc.psum_pool(name="psum", bufs=8))
         ctx.enter_context(tc.manual_schedule())
@@ -79,13 +81,15 @@ def tile_conv2d_kernel(tc, x, K, out):
         def prep_chunk(c):
             b, r0, r1 = CHUNKS[c]
             ra, rb = r0 + 1, r1 + 1
-            dst = g[1][:, ra * W : rb * W, :].rearrange("p (c i) t -> p c t i", i=4)
-            src = raw[c][:].rearrange("p t (c i) -> p c t i", i=4)
             last = (W - 1) * PACK
-            if c == 0:
-                nc.vector.tensor_copy(out=dst, in_=src)
-            else:
-                nc.scalar.copy(out=dst, in_=src)
+            cuts = [0, (r1 - r0) // 2, r1 - r0] if c == 0 else [0, r1 - r0]
+            for a0, a1 in zip(cuts[:-1], cuts[1:]):
+                dst = g[1][:, (ra + a0) * W : (ra + a1) * W, :].rearrange("p (c i) t -> p c t i", i=4)
+                src = raw[c][:, :, a0 * W : a1 * W].rearrange("p t (c i) -> p c t i", i=4)
+                if c == 0:
+                    nc.vector.tensor_copy(out=dst, in_=src)
+                else:
+                    nc.scalar.copy(out=dst, in_=src)
             nc.scalar.copy(out=gword[0][:, ra:rb, 2:], in_=gword[1][:, ra:rb, 0 : last // 2])
             nc.scalar.copy(out=gword[2][:, ra:rb, 0 : last // 2], in_=gword[1][:, ra:rb, 2:])
 
@@ -93,11 +97,22 @@ def tile_conv2d_kernel(tc, x, K, out):
         kw = keep.tile([P, TAPS * C_OUT], U32, align_bytes=64, name="kw")
         ks = keep.tile([P, TAPS * C_OUT], U8, align_bytes=64, name="ks")
 
-        def prep_weights():
+        def interleave_weights():
             nc.vector.tensor_copy(
                 out=kg[:].rearrange("p (c i) t -> p c t i", i=4),
                 in_=kraw[:].rearrange("p t (c i) -> p c t i", i=4),
             )
+            warm = psum.tile([P, BANK], F32, tag="acc", name="warm")
+            for i in range(WARM_UP):
+                nc.tensor.matmul(
+                    warm[:],
+                    lhsT=kg[:, 0 : C_OUT // PACK, :].rearrange("p c t -> p (c t)"),
+                    rhs=kg[:, 0 : BANK // PACK, :].rearrange("p c t -> p (c t)"),
+                    start=True,
+                    stop=True,
+                )
+
+        def quantise_weights():
             for c0, c1 in ((0, 1024), (1024, 1152)):
                 nc.vector.quantize_mx(
                     out=kw[:, c0:c1].bitcast(FP8X4),
@@ -176,9 +191,13 @@ def tile_conv2d_kernel(tc, x, K, out):
 
         def head_quantise(c0, n):
             quantise_at = LEFT + c0
+            for idx in range(CENTRE_TAPS):
+                left_quantise(0, 0, idx)
             for idx in range(TAPS):
-                if c0 == 0:
+                if idx >= CENTRE_TAPS:
                     left_quantise(0, 0, idx)
+                if idx == TAPS - 1:
+                    interleave_weights()
                 quantise(hw[:, idx, c0 : c0 + n], hs[:, idx, c0 : c0 + n], TAP_ORDER[idx], quantise_at, n)
 
         def head_multiply():
@@ -253,7 +272,7 @@ def tile_conv2d_kernel(tc, x, K, out):
             if kind == "head":
                 head_quantise(q0 - LEFT, n)
                 if i == len(HEAD) - 1:
-                    prep_weights()
+                    quantise_weights()
                     head_multiply()
             elif kind == "group":
                 group(b, q0, n)

@@ -10,6 +10,7 @@ FP8X4 = mybir.dt.float8_e4m3fn_x4
 
 P = 128
 PACK = 4
+RUN = 8
 NB = 2
 C_OUT = 128
 H = 56
@@ -31,9 +32,9 @@ FLOPS = 2 * NB * NPX * 512 * TAPS * C_OUT
 TAP_ORDER = [1, 4, 7, 0, 3, 6, 2, 5, 8]
 HEAD = [256]
 GROUPS_B0 = [512, 256, 1024, 1024]
-GROUPS_B1 = [1024, 1024]
-LAST = 1024
-LAST_PIECE = 256
+GROUPS_B1 = [1024, 1024, 512]
+LAST = 512
+LAST_PIECE = 128
 WARM_UP = 3
 LEFT = 64
 CENTRE_TAPS = 3
@@ -84,8 +85,8 @@ def tile_conv2d_kernel(tc, x, K, out):
             last = (W - 1) * PACK
             cuts = [0, (r1 - r0) // 2, r1 - r0] if c == 0 else [0, r1 - r0]
             for a0, a1 in zip(cuts[:-1], cuts[1:]):
-                dst = g[1][:, (ra + a0) * W : (ra + a1) * W, :].rearrange("p (c i) t -> p c t i", i=4)
-                src = raw[c][:, :, a0 * W : a1 * W].rearrange("p t (c i) -> p c t i", i=4)
+                dst = g[1][:, (ra + a0) * W : (ra + a1) * W, :].rearrange("p (c i) t -> p c t i", i=RUN)
+                src = raw[c][:, :, a0 * W : a1 * W].rearrange("p t (c i) -> p c t i", i=RUN)
                 if c == 0:
                     nc.vector.tensor_copy(out=dst, in_=src)
                 else:
@@ -99,8 +100,8 @@ def tile_conv2d_kernel(tc, x, K, out):
 
         def interleave_weights():
             nc.vector.tensor_copy(
-                out=kg[:].rearrange("p (c i) t -> p c t i", i=4),
-                in_=kraw[:].rearrange("p t (c i) -> p c t i", i=4),
+                out=kg[:].rearrange("p (c i) t -> p c t i", i=RUN),
+                in_=kraw[:].rearrange("p t (c i) -> p c t i", i=RUN),
             )
             warm = psum.tile([P, BANK], F32, tag="acc", name="warm")
             for i in range(WARM_UP):

from contextlib import ExitStack

import concourse.mybir as mybir

BF16 = mybir.dt.bfloat16
F32 = mybir.dt.float32
U32 = mybir.dt.uint32
U8 = mybir.dt.uint8
FP8X4 = mybir.dt.float8_e4m3fn_x4

P = 128
PACK = 4
RUN = 8
NB = 2
C_OUT = 128
H = 56
W = 56
RP = H + 2
NPX = H * W
TAPS = 9
ROWS_B0 = [8, 8, 8, 16, 16]
ROWS_B1 = [8, 16, 16, 16]
CHUNKS = [
    (b, sum(rows[:i]), sum(rows[: i + 1])) for b, rows in enumerate((ROWS_B0, ROWS_B1)) for i in range(len(rows))
]
LEAD_ROWS = 24
KEEP_BANKS = 4
BANK = 512

FLOPS = 2 * NB * NPX * 512 * TAPS * C_OUT

TAP_ORDER = [1, 4, 7, 0, 3, 6, 2, 5, 8]
HEAD = [256]
GROUPS_B0 = [512, 256, 1024, 1024]
GROUPS_B1 = [1024, 1024, 512]
LAST = 512
LAST_PIECE = 128
WARM_UP = 3
LEFT = 64
CENTRE_TAPS = 3


def tile_conv2d_kernel(tc, x, K, out):
    nc = tc.nc
    with ExitStack() as ctx:
        keep = ctx.enter_context(tc.tile_pool(name="keep", bufs=1))
        wpool = ctx.enter_context(tc.tile_pool(name="wpool", bufs=10))
        opool = ctx.enter_context(tc.tile_pool(name="opool", bufs=4))
        psum = ctx.enter_context(tc.psum_pool(name="psum", bufs=8))
        ctx.enter_context(tc.manual_schedule())

        raw = {}
        kraw = keep.tile([P, PACK, TAPS * C_OUT], BF16, name="kraw")

        def load_chunk(c):
            b, r0, r1 = CHUNKS[c]
            t = keep.tile([P, PACK, (r1 - r0) * W], BF16, name="raw%d" % c)
            nc.sync.dma_start(
                out=t[:],
                in_=x[b, :, r0:r1, :].rearrange("(p t) r c -> p t (r c)", t=PACK),
            )
            raw[c] = t

        load_chunk(0)
        load_chunk(1)
        nc.sync.dma_start(
            out=kraw[:].rearrange("p t f -> p (t f)"),
            in_=K.rearrange("a b c o -> (a b c) o").rearrange("(p f) o -> p (f o)", p=P),
        )
        for c in range(2, len(CHUNKS)):
            load_chunk(c)

        g = [keep.tile([P, RP * W, PACK], BF16, align_bytes=64, name="g%d" % dj) for dj in range(3)]
        grow = [t[:].rearrange("p (r j) t -> p r (j t)", j=W) for t in g]
        gword = [t[:].rearrange("p q t -> p (q t)").bitcast(F32).rearrange("p (r v) -> p r v", r=RP) for t in g]
        for dj in (1, 0, 2):
            nc.vector.memset(grow[dj][:, 0:1, :], 0.0)
            nc.vector.memset(grow[dj][:, RP - 1 : RP, :], 0.0)
        nc.gpsimd.memset(grow[0][:, 1 : RP - 1, 0:PACK], 0.0)
        nc.gpsimd.memset(grow[2][:, 1 : RP - 1, (W - 1) * PACK : W * PACK], 0.0)

        def prep_chunk(c):
            b, r0, r1 = CHUNKS[c]
            ra, rb = r0 + 1, r1 + 1
            last = (W - 1) * PACK
            cuts = [0, (r1 - r0) // 2, r1 - r0] if c == 0 else [0, r1 - r0]
            for a0, a1 in zip(cuts[:-1], cuts[1:]):
                dst = g[1][:, (ra + a0) * W : (ra + a1) * W, :].rearrange("p (c i) t -> p c t i", i=RUN)
                src = raw[c][:, :, a0 * W : a1 * W].rearrange("p t (c i) -> p c t i", i=RUN)
                if c == 0:
                    nc.vector.tensor_copy(out=dst, in_=src)
                else:
                    nc.scalar.copy(out=dst, in_=src)
            nc.scalar.copy(out=gword[0][:, ra:rb, 2:], in_=gword[1][:, ra:rb, 0 : last // 2])
            nc.scalar.copy(out=gword[2][:, ra:rb, 0 : last // 2], in_=gword[1][:, ra:rb, 2:])

        kg = keep.tile([P, TAPS * C_OUT, PACK], BF16, align_bytes=64, name="kg")
        kw = keep.tile([P, TAPS * C_OUT], U32, align_bytes=64, name="kw")
        ks = keep.tile([P, TAPS * C_OUT], U8, align_bytes=64, name="ks")

        def interleave_weights():
            nc.vector.tensor_copy(
                out=kg[:].rearrange("p (c i) t -> p c t i", i=RUN),
                in_=kraw[:].rearrange("p t (c i) -> p c t i", i=RUN),
            )
            warm = psum.tile([P, BANK], F32, tag="acc", name="warm")
            for i in range(WARM_UP):
                nc.tensor.matmul(
                    warm[:],
                    lhsT=kg[:, 0 : C_OUT // PACK, :].rearrange("p c t -> p (c t)"),
                    rhs=kg[:, 0 : BANK // PACK, :].rearrange("p c t -> p (c t)"),
                    start=True,
                    stop=True,
                )

        def quantise_weights():
            for c0, c1 in ((0, 1024), (1024, 1152)):
                nc.vector.quantize_mx(
                    out=kw[:, c0:c1].bitcast(FP8X4),
                    scales=ks[:, c0:c1],
                    in_=kg[:, c0:c1, :].rearrange("p c t -> p (c t)"),
                )

        def quantise(dst_w, dst_s, s, q0, n):
            di, dj = divmod(s, 3)
            a = q0 + W * di
            nc.vector.quantize_mx(
                out=dst_w.bitcast(FP8X4),
                scales=dst_s,
                in_=g[dj][:, a : a + n, :].rearrange("p q t -> p (q t)"),
            )

        def multiply(acc, src_w, src_s, idx):
            s = TAP_ORDER[idx]
            nc.tensor.matmul_mx(
                out=acc,
                lhsT=kw[:, s * C_OUT : (s + 1) * C_OUT].bitcast(FP8X4),
                lhsT_scale=ks[:, s * C_OUT : (s + 1) * C_OUT],
                rhs=src_w.bitcast(FP8X4),
                rhs_scale=src_s,
                start=(idx == 0),
                stop=(idx == TAPS - 1),
            )

        out_flat = [out[b].rearrange("o i j -> o (i j)") for b in range(NB)]

        pending = []
        flushed = [0]

        def finish(acc, n, pieces):
            pending.append((acc, n, pieces))

        def flush(keep_last):
            while len(pending) - flushed[0] > keep_last:
                acc, n, pieces = pending[flushed[0]]
                flushed[0] += 1
                res = opool.tile([P, n], F32, tag="res", name="res")
                nc.scalar.copy(out=res[:], in_=acc[:])
                for b, q0, c0, m in pieces:
                    nc.sync.dma_start(out=out_flat[b][:, q0 : q0 + m], in_=res[:, c0 : c0 + m])

        def group(b, q0, n):
            width = min(n, BANK)
            accs = [psum.tile([P, width], F32, tag="acc", name="acc%d" % h) for h in range(n // width)]
            for idx in range(TAPS):
                w = wpool.tile([P, n], U32, align_bytes=64, tag="w", name="w")
                sc = wpool.tile([P, n], U8, align_bytes=64, tag="sc", name="sc")
                quantise(w[:], sc[:], TAP_ORDER[idx], q0, n)
                for h, acc in enumerate(accs):
                    multiply(acc[:], w[:, h * width : (h + 1) * width], sc[:, h * width : (h + 1) * width], idx)
            for h, acc in enumerate(accs):
                finish(acc, width, [(b, q0 + h * width, 0, width)])

        def last_group(b, q0):
            accs = [psum.tile([P, LAST_PIECE], F32, tag="acc", name="accz%d" % h) for h in range(LAST // LAST_PIECE)]
            for idx in range(TAPS):
                w = wpool.tile([P, LAST], U32, align_bytes=64, tag="w", name="w")
                sc = wpool.tile([P, LAST], U8, align_bytes=64, tag="sc", name="sc")
                if idx < TAPS - 1:
                    quantise(w[:], sc[:], TAP_ORDER[idx], q0, LAST)
                for h, acc in enumerate(accs):
                    c0, c1 = h * LAST_PIECE, (h + 1) * LAST_PIECE
                    if idx == TAPS - 1:
                        quantise(w[:, c0:c1], sc[:, c0:c1], TAP_ORDER[idx], q0 + c0, LAST_PIECE)
                    multiply(acc[:], w[:, c0:c1], sc[:, c0:c1], idx)
            for h, acc in enumerate(accs):
                finish(acc, LAST_PIECE, [(b, q0 + h * LAST_PIECE, 0, LAST_PIECE)])

        n_head = sum(HEAD)
        hw = keep.tile([P, TAPS, n_head], U32, align_bytes=64, name="hw")
        hs = keep.tile([P, TAPS, n_head], U8, align_bytes=64, name="hs")

        def head_quantise(c0, n):
            quantise_at = LEFT + c0
            for idx in range(CENTRE_TAPS):
                left_quantise(0, 0, idx)
            for idx in range(TAPS):
                if idx >= CENTRE_TAPS:
                    left_quantise(0, 0, idx)
                if idx == TAPS - 1:
                    interleave_weights()
                quantise(hw[:, idx, c0 : c0 + n], hs[:, idx, c0 : c0 + n], TAP_ORDER[idx], quantise_at, n)

        def head_multiply():
            c0 = 0
            for n in HEAD:
                acc = psum.tile([P, n], F32, tag="acc", name="acch")
                for idx in range(TAPS):
                    multiply(acc[:], hw[:, idx, c0 : c0 + n], hs[:, idx, c0 : c0 + n], idx)
                finish(acc, n, [(0, LEFT + c0, 0, n)])
                c0 += n

        lw = keep.tile([P, TAPS, 2 * LEFT], U32, align_bytes=64, name="lw")
        ls = keep.tile([P, TAPS, 2 * LEFT], U8, align_bytes=64, name="ls")

        def left_quantise(b, q0, idx):
            quantise(
                lw[:, idx, b * LEFT : (b + 1) * LEFT], ls[:, idx, b * LEFT : (b + 1) * LEFT], TAP_ORDER[idx], q0, LEFT
            )

        def left_finish():
            acc = psum.tile([P, 2 * LEFT], F32, tag="acc", name="accl")
            for idx in range(TAPS):
                multiply(acc[:], lw[:, idx, :], ls[:, idx, :], idx)
            finish(acc, 2 * LEFT, [(b, 0, b * LEFT, LEFT) for b in range(NB)])

        work = []
        q = LEFT
        for n in HEAD:
            work.append(("head", 0, q, n))
            q += n
        for n in GROUPS_B0:
            work.append(("group", 0, q, n))
            q += n
        assert q == NPX
        work.append(("left", 1, 0, LEFT))
        q = LEFT
        for n in GROUPS_B1:
            work.append(("group", 1, q, n))
            q += n
        work.append(("last", 1, q, LAST))
        assert q + LAST == NPX

        def chunk_of_row(b, row):
            for c, (cb, r0, r1) in enumerate(CHUNKS):
                if (cb, r1) > (b, row):
                    return c
            return len(CHUNKS) - 1

        def last_row_needed(q0, n):
            return min(H - 1, (q0 + n - 1) // W + 1)

        def first_free_index(c):
            cb, r0, r1 = CHUNKS[c]
            idx = 0
            for i, (kind, b, q0, n) in enumerate(work):
                if cb == 1 and b == 0 and q0 // W <= r1:
                    idx = i + 1
            return idx

        def ahead(b, row):
            b, row = b + (row + LEAD_ROWS) // H, (row + LEAD_ROWS) % H
            return chunk_of_row(b, row) if b < NB else len(CHUNKS) - 1

        done = 0
        for i, (kind, b, q0, n) in enumerate(work):
            row = last_row_needed(q0, n)
            need = chunk_of_row(b, row)
            while done <= ahead(b, row) and done < len(CHUNKS) and first_free_index(done) <= i:
                prep_chunk(done)
                done += 1
            assert done > need
            if kind == "head":
                head_quantise(q0 - LEFT, n)
                if i == len(HEAD) - 1:
                    quantise_weights()
                    head_multiply()
            elif kind == "group":
                group(b, q0, n)
            elif kind == "left":
                for idx in range(TAPS):
                    left_quantise(b, q0, idx)
                left_finish()
            else:
                last_group(b, q0)
            flush(KEEP_BANKS)
        flush(0)
